import numpy as np
import ml_dtypes


def mxq(x, axis, fmt="e4m3"):
    dtype, down = {"e4m3": (ml_dtypes.float8_e4m3fn, 7), "e5m2": (ml_dtypes.float8_e5m2, 14)}[fmt]
    v = np.moveaxis(np.asarray(x, np.float32).astype(ml_dtypes.bfloat16).astype(np.float64), axis, -1)
    blocks = v.reshape(v.shape[:-1] + (-1, 32))
    amax = np.abs(blocks).max(-1, keepdims=True)
    byte = np.maximum(np.where(amax > 0, np.frexp(amax)[1] - 1 + 127, 0) - down, 1)
    scale = np.exp2(byte - 127.0)
    codes = (blocks / scale).astype(np.float32).astype(dtype).astype(np.float64)
    return np.moveaxis((codes * scale).reshape(v.shape), -1, axis)


WIDE = False


def mx_kscale(k):
    if not WIDE:
        return np.ones(k)
    levels = np.array([10, -10, 5, -5, 0])
    a = np.random.permutation(np.resize(levels, k // 512 * 4)).reshape(k // 512, 4)
    idx = np.arange(k)
    return np.exp2(a[idx // 512, idx % 128 // 32])


BF16 = ml_dtypes.bfloat16


def bf(x):
    return np.asarray(x, np.float32).astype(BF16)


def f64(x):
    return np.asarray(x).astype(np.float64)


B, CH, C1, C2, D, NF, W, H = 2, 128, 128, 512, 2, 16, 16, 16
N = NF * W * H
M = NF * (W // D) * (H // D)


def setup_inputs():
    t = mx_kscale(C2)
    return {"theta": bf(np.tanh(np.random.standard_normal((B, N, C1)) * 0.3)),
            "phi": bf(np.tanh(0.3 + np.random.standard_normal((B, M, C1)) * 0.2)),
            "g": bf((1.0 + np.random.standard_normal((B, M, C2)) * 0.7) * t),
            "x": bf(np.random.standard_normal((B, CH, NF, W, H))),
            "w_attn_g": bf(np.random.standard_normal((CH, C2)) * 2.0 / np.sqrt(C2) / t),
            "b_attn_g": bf(np.random.standard_normal(CH) * 0.2),
            "gamma": bf(0.6 + np.random.standard_normal(1) * 0.2)}


def reference(theta, phi, g, x, w_attn_g, b_attn_g, gamma):
    s = f64(theta) @ f64(phi).transpose(0, 2, 1)
    e = np.exp(s - s.max(axis=1, keepdims=True))
    attn = e / e.sum(axis=1, keepdims=True)
    a = mxq(attn, 2, "e4m3") @ mxq(f64(g), 1, "e4m3")
    y = (mxq(f64(w_attn_g), 1, "e4m3") @ mxq(a.transpose(0, 2, 1), 1, "e4m3")) + f64(b_attn_g)[None, :, None]
    attn_g = y.reshape(B, CH, NF, W, H)
    alpha = 1.0 / (1.0 + np.exp(-f64(gamma)[0]))
    out = (1.0 - alpha) * f64(x) + alpha * attn_g
    return out, attn_g

@@ -1,0 +1,446 @@
+from contextlib import ExitStack
+
+import concourse.masks as masks
+import concourse.mybir as mybir
+
+F32 = mybir.dt.float32
+BF16 = mybir.dt.bfloat16
+U32 = mybir.dt.uint32
+U8 = mybir.dt.uint8
+FP8X4 = mybir.dt.float8_e4m3fn_x4
+ALU = mybir.AluOpType
+ACT = mybir.ActivationFunctionType
+AX = mybir.AxisListType
+
+P = 128
+B = 2
+NQ = 4096
+NK = 1024
+C1 = 128
+C2 = 512
+CH = 128
+NCH = 512
+NCHUNK = NQ // NCH
+NSTEP = 4 * NCHUNK
+
+FLOPS = 2 * B * (NQ * NK * C1 + NQ * NK * C2 + CH * C2 * NQ)
+
+MANUAL = True
+E_BUFS = 10
+S_BANKS = 5
+G_REGROUP = "G"
+XS_ENGINE = "G"
+
+
+def norm_engine(gi, c):
+    return "A" if (c == 0 or gi == 1) else ("SSSv" if gi != 3 else "A")
+
+
+def tile_selfattention3d_pa_t_kernel(tc, theta, phi, g, x, w_attn_g, b_attn_g, gamma, out_0, out_1):
+    nc = tc.nc
+    with ExitStack() as ctx:
+        if MANUAL:
+            ctx.enter_context(tc.manual_schedule())
+        const = ctx.enter_context(tc.tile_pool(name="const", bufs=1))
+        raw = ctx.enter_context(tc.tile_pool(name="raw", bufs=3))
+        graw_pool = ctx.enter_context(tc.tile_pool(name="graw", bufs=2))
+        gg_pool = ctx.enter_context(tc.tile_pool(name="gg", bufs=2))
+        e_pool = ctx.enter_context(tc.tile_pool(name="e", bufs=E_BUFS))
+        st_pool = ctx.enter_context(tc.tile_pool(name="st", bufs=2))
+        pl_pool = ctx.enter_context(tc.tile_pool(name="pl", bufs=2))
+        grp_pool = ctx.enter_context(tc.tile_pool(name="grp", bufs=2))
+        cod0_pool = ctx.enter_context(tc.tile_pool(name="cod0", bufs=8))
+        cod1_pool = ctx.enter_context(tc.tile_pool(name="cod1", bufs=3))
+        a_pool = ctx.enter_context(tc.tile_pool(name="a", bufs=2))
+        x_pool = ctx.enter_context(tc.tile_pool(name="x", bufs=6))
+        io_pool = ctx.enter_context(tc.tile_pool(name="io", bufs=2))
+        ps_s = ctx.enter_context(tc.psum_pool(name="ps_s", bufs=S_BANKS))
+        ps_a = ctx.enter_context(tc.psum_pool(name="ps_a", bufs=2))
+        ps_y = ctx.enter_context(tc.psum_pool(name="ps_y", bufs=1))
+
+        th_v = [theta[b].rearrange("(r p) c -> p r c", p=P) for b in range(B)]
+        ph_v = [phi[b].rearrange("(g p t) c -> p g t c", g=2, p=P, t=4) for b in range(B)]
+        g_v = [g[b].rearrange("(g p j) c -> p g j c", g=2, p=P, j=4) for b in range(B)]
+        x_v = [x[b].rearrange("c f w h -> c (f w h)") for b in range(B)]
+        o0_v = [out_0[b].rearrange("c f w h -> c (f w h)") for b in range(B)]
+        o1_v = [out_1[b].rearrange("c f w h -> c (f w h)") for b in range(B)]
+
+        ident = const.tile([P, P], BF16, name="ident")
+        masks.make_identity(nc, ident[:])
+
+        thetaT = [const.tile([P, NQ], BF16, name="thetaT%d" % b) for b in range(B)]
+        nphiT = [const.tile([P, 8, P], BF16, name="nphiT%d" % b) for b in range(B)]
+        gcod = [const.tile([P, C2], U32, name="gcod%d" % i, align_bytes=64) for i in range(4)]
+        gpl = [const.tile([P, C2], U8, name="gpl%d" % i, align_bytes=64) for i in range(4)]
+        wcod = const.tile([P, CH], U32, name="wcod", align_bytes=64)
+        wpl = const.tile([P, CH], U8, name="wpl", align_bytes=64)
+        praw = [const.tile([P, 2, 4, C1], BF16, name="praw%d" % b) for b in range(B)]
+        wraw = const.tile([P, C2], BF16, name="wraw")
+        gam = const.tile([P, 1], BF16, name="gam")
+        braw = const.tile([P, 1], BF16, name="braw")
+        alpha = const.tile([P, 1], F32, name="alpha")
+        oma = const.tile([P, 1], F32, name="oma")
+        b32 = const.tile([P, 1], F32, name="b32")
+
+        traws = {}
+        graws = {}
+        ggs = {}
+
+        def load_theta(b, q):
+            traw = raw.tile([P, 8, C1], BF16, name="traw", tag="traw")
+            nc.sync.dma_start(out=traw[:], in_=th_v[b][:, 8 * q:8 * q + 8, :])
+            traws[(b, q)] = traw
+
+        def load_g(i):
+            gr = graw_pool.tile([P, 4, C2], BF16, name="gr", tag="gr")
+            nc.sync.dma_start(out=gr[:], in_=g_v[i // 2][:, i % 2, :, :])
+            graws[i] = gr
+
+        pts = {}
+
+        def transpose_phi(b, h):
+            pt = ps_a.tile([P, 4, P], BF16, name="pt", tag="a")
+            for i in range(4):
+                nc.tensor.transpose(pt[:, i, :], praw[b][:, h, i, :], ident[:])
+            pts[("phi", b, h)] = pt
+
+        def evac_phi(b, h):
+            nc.vector.tensor_scalar_mul(out=nphiT[b][:, 4 * h:4 * h + 4, :], in0=pts[("phi", b, h)][:], scalar1=-1.0)
+
+        def transpose_theta(b, i4):
+            q, h = divmod(i4, 2)
+            traw = traws[(b, q)]
+            pt = ps_a.tile([P, 4, P], BF16, name="pt", tag="a")
+            for i in range(4):
+                nc.tensor.transpose(pt[:, i, :], traw[:, 4 * h + i, :], ident[:])
+            pts[("theta", b, i4)] = pt
+
+        def evac_theta(b, i4, use_vector):
+            pt = pts[("theta", b, i4)]
+            dst = thetaT[b][:, i4 * NCH:(i4 + 1) * NCH]
+            if use_vector:
+                nc.vector.tensor_copy(out=dst, in_=pt[:].rearrange("p i n -> p (i n)"))
+            else:
+                nc.scalar.copy(out=dst, in_=pt[:].rearrange("p i n -> p (i n)"))
+
+        def regroup_g(i):
+            gg = gg_pool.tile([P, C2, 4], BF16, name="gg", tag="gg", align_bytes=64)
+            dst = gg[:].rearrange("p (c i) t -> p c t i", i=4)
+            srcv = graws[i][:].rearrange("p t (c i) -> p c t i", i=4)
+            if G_REGROUP == "G":
+                nc.gpsimd.tensor_scalar(out=dst, in0=srcv, scalar1=1.0, scalar2=0.0, op0=ALU.mult, op1=ALU.add)
+            else:
+                nc.vector.tensor_copy(out=dst, in_=srcv)
+            ggs[i] = gg
+
+        def quant_g(i):
+            nc.vector.quantize_mx(out=gcod[i][:].bitcast(FP8X4), scales=gpl[i][:],
+                                  in_=ggs[i][:].rearrange("p c t -> p (c t)"))
+
+        eg = const.tile([P, 1], F32, name="eg")
+
+        def small_constants_s():
+            nc.scalar.activation(out=eg[:], in_=gam[:], func=ACT.Exp, scale=-1.0)
+
+        def small_constants_v():
+            den = const.tile([P, 1], F32, name="den")
+            nc.vector.tensor_scalar_add(out=den[:], in0=eg[:], scalar1=1.0)
+            nc.vector.reciprocal(out=alpha[:], in_=den[:])
+            nc.vector.tensor_scalar(out=oma[:], in0=alpha[:], scalar1=-1.0, scalar2=1.0, op0=ALU.mult, op1=ALU.add)
+            nc.vector.tensor_copy(out=b32[:], in_=braw[:])
+
+        wgs = {}
+
+        def transpose_w():
+            wt = ps_y.tile([P, 4, P], BF16, name="wt", tag="y")
+            for j in range(4):
+                nc.tensor.transpose(wt[:, j, :], wraw[:, j * P:(j + 1) * P], ident[:])
+            wgs[1] = wt
+
+        def evac_w():
+            wg = const.tile([P, CH, 4], BF16, name="wg", align_bytes=64)
+            nc.vector.tensor_copy(out=wg[:], in_=wgs[1][:].rearrange("p j c -> p c j"))
+            wgs[0] = wg
+
+        def quant_w():
+            nc.vector.quantize_mx(out=wcod[:].bitcast(FP8X4), scales=wpl[:],
+                                  in_=wgs[0][:].rearrange("p c j -> p (c j)"))
+
+        ps_tiles = {}
+        e_tiles = {}
+        nm_tiles = {}
+        sm_tiles = {}
+        f_tiles = {}
+        sc_tiles = {}
+        pl_tiles = {}
+        grp_tiles = {}
+        cod_tiles = {}
+        pa_tiles = {}
+        agrp_tiles = {}
+        acod_tiles = {}
+        py_tiles = {}
+        xc_tiles = {}
+        xs_tiles = {}
+        ag_tiles = {}
+
+        def issue_s(k, t):
+            gi, c = divmod(k, NCHUNK)
+            b, gp = divmod(gi, 2)
+            ps = ps_s.tile([P, NCH], F32, name="ps", tag="s")
+            nc.tensor.matmul(ps[:], lhsT=nphiT[b][:, gp * 4 + t, :], rhs=thetaT[b][:, c * NCH:(c + 1) * NCH],
+                             start=True, stop=True)
+            ps_tiles[(k, t)] = ps
+
+        def red_exp(k, t):
+            gi, c = divmod(k, NCHUNK)
+            if c == 0 and t == 0:
+                nm_tiles[gi] = st_pool.tile([P, 4, NCHUNK], F32, name="nm", tag="nm")
+                sm_tiles[gi] = st_pool.tile([P, 4, NCHUNK], F32, name="sm", tag="sm")
+            if t == 0:
+                e_tiles[k] = e_pool.tile([P, 4, NCH], F32, name="e", tag="e")
+            ps = ps_tiles[(k, t)]
+            nm = nm_tiles[gi]
+            nc.vector.tensor_reduce(out=nm[:, t, c:c + 1], in_=ps[:], axis=AX.X, op=ALU.min)
+            nc.scalar.activation(out=e_tiles[k][:, t, :], in_=ps[:], func=ACT.Exp, bias=nm[:, t, c:c + 1], scale=-1.0,
+                                 accum_out=sm_tiles[gi][:, t, c:c + 1])
+
+        def stats1(gi):
+            nm = nm_tiles[gi]
+            negm = st_pool.tile([P, 4], F32, name="negm", tag="negm")
+            nc.vector.tensor_reduce(out=negm[:], in_=nm[:], axis=AX.X, op=ALU.min)
+            d = st_pool.tile([P, 4, NCHUNK], F32, name="d", tag="d")
+            nc.vector.tensor_tensor(out=d[:], in0=negm[:].unsqueeze(2).to_broadcast([P, 4, NCHUNK]), in1=nm[:],
+                                    op=ALU.subtract)
+            f = st_pool.tile([P, 4, NCHUNK], F32, name="f", tag="f")
+            nc.scalar.activation(out=f[:], in_=d[:], func=ACT.Exp)
+            f_tiles[gi] = f
+
+        def stats2(gi):
+            f = f_tiles[gi]
+            fs = st_pool.tile([P, 4, NCHUNK], F32, name="fs", tag="fs")
+            nc.vector.tensor_tensor(out=fs[:], in0=f[:], in1=sm_tiles[gi][:], op=ALU.mult)
+            tot = st_pool.tile([P, 4], F32, name="tot", tag="tot")
+            nc.vector.tensor_reduce(out=tot[:], in_=fs[:], axis=AX.X, op=ALU.add)
+            r = st_pool.tile([P, 4], F32, name="r", tag="r")
+            nc.vector.reciprocal(out=r[:], in_=tot[:])
+            sc = st_pool.tile([P, 4, NCHUNK], F32, name="sc", tag="sc")
+            nc.vector.tensor_tensor(out=sc[:], in0=f[:], in1=r[:].unsqueeze(2).to_broadcast([P, 4, NCHUNK]),
+                                    op=ALU.mult)
+            sc_tiles[gi] = sc
+
+        def planes(j, who):
+            gi, c = divmod(j, NCHUNK)
+            eng = norm_engine(gi, c)
+            if eng == "A":
+                return
+            if j not in pl_tiles:
+                pl_tiles[j] = pl_pool.tile([P, 4, NCH], BF16, name="pl", tag="pl")
+            pl = pl_tiles[j]
+            e = e_tiles[j]
+            sc = sc_tiles[gi]
+            for t in range(4):
+                if eng[t] not in who:
+                    continue
+                if eng[t] == "S":
+                    nc.scalar.activation(out=pl[:, t, :], in_=e[:, t, :], func=ACT.Copy, scale=sc[:, t, c:c + 1])
+                elif eng[t] == "G":
+                    nc.gpsimd.tensor_scalar(out=pl[:, t, :], in0=e[:, t, :], scalar1=sc[:, t, c:c + 1],
+                                            scalar2=0.0, op0=ALU.mult, op1=ALU.add)
+                else:
+                    nc.vector.tensor_scalar_mul(out=pl[:, t, :], in0=e[:, t, :], scalar1=sc[:, t, c:c + 1])
+
+        def normalise(j):
+            gi, c = divmod(j, NCHUNK)
+            grp = grp_pool.tile([P, NCH, 4], BF16, name="grp", tag="grp", align_bytes=64)
+            if norm_engine(gi, c) == "A":
+                nc.vector.tensor_tensor(
+                    out=grp[:].rearrange("p (c i) t -> p c t i", i=4),
+                    in0=e_tiles[j][:].rearrange("p t (c i) -> p c t i", i=4),
+                    in1=sc_tiles[gi][:, :, c:c + 1].unsqueeze(1).to_broadcast([P, NCH // 4, 4, 4]),
+                    op=ALU.mult,
+                )
+            else:
+                nc.vector.tensor_copy(
+                    out=grp[:].rearrange("p (c i) t -> p c t i", i=4),
+                    in_=pl_tiles[j][:].rearrange("p t (c i) -> p c t i", i=4),
+                )
+            grp_tiles[j] = grp
+
+        def quantise(j):
+            gi, c = divmod(j, NCHUNK)
+            pool = cod0_pool if gi % 2 == 0 else cod1_pool
+            cod = pool.tile([P, NCH], U32, name="cod", tag="cod", align_bytes=64)
+            pln = pool.tile([P, NCH], U8, name="pln", tag="pln", align_bytes=64)
+            nc.vector.quantize_mx(out=cod[:].bitcast(FP8X4), scales=pln[:],
+                                  in_=grp_tiles[j][:].rearrange("p n t -> p (n t)"))
+            cod_tiles[j] = (cod, pln)
+
+        def a_mm(j, sub):
+            b = j // (2 * NCHUNK)
+            ops = [cod_tiles[j - NCHUNK], cod_tiles[j]]
+            pa = ps_a.tile([P, 4, P], F32, name="pa", tag="a")
+            cols = slice(sub * P, (sub + 1) * P)
+            for jj in range(4):
+                mcols = slice(jj * P, (jj + 1) * P)
+                for gp in range(2):
+                    nc.tensor.matmul_mx(
+                        out=pa[:, jj, :],
+                        lhsT=gcod[2 * b + gp][:, mcols].bitcast(FP8X4),
+                        lhsT_scale=gpl[2 * b + gp][:, mcols],
+                        rhs=ops[gp][0][:, cols].bitcast(FP8X4),
+                        rhs_scale=ops[gp][1][:, cols],
+                        start=(gp == 0),
+                        stop=(gp == 1),
+                    )
+            pa_tiles[(j, sub)] = pa
+
+        def a_evac(j, sub):
+            if sub == 0:
+                agrp_tiles[j] = a_pool.tile([P, NCH, 4], BF16, name="agrp", tag="agrp", align_bytes=64)
+            nc.scalar.copy(out=agrp_tiles[j][:, sub * P:(sub + 1) * P, :],
+                           in_=pa_tiles[(j, sub)][:].rearrange("p j n -> p n j"))
+
+        def a_quant(j):
+            acod = a_pool.tile([P, NCH], U32, name="acod", tag="acod", align_bytes=64)
+            apl = a_pool.tile([P, NCH], U8, name="apl", tag="apl", align_bytes=64)
+            nc.vector.quantize_mx(out=acod[:].bitcast(FP8X4), scales=apl[:],
+                                  in_=agrp_tiles[j][:].rearrange("p n t -> p (n t)"))
+            acod_tiles[j] = (acod, apl)
+
+        def out_cols(j):
+            c = j % NCHUNK
+            return j // (2 * NCHUNK), slice(c * NCH, (c + 1) * NCH)
+
+        def x_load(j):
+            b, cols = out_cols(j)
+            xc = x_pool.tile([P, NCH], BF16, name="xc", tag="xc")
+            nc.sync.dma_start(out=xc[:], in_=x_v[b][:, cols])
+            xc_tiles[j] = xc
+
+        def x_scale(j):
+            xs = io_pool.tile([P, NCH], F32, name="xs", tag="xs", bufs=3)
+            if XS_ENGINE == "G":
+                nc.gpsimd.tensor_scalar(out=xs[:], in0=xc_tiles[j][:], scalar1=oma[:, 0:1], scalar2=0.0, op0=ALU.mult,
+                                        op1=ALU.add)
+            else:
+                nc.vector.tensor_scalar_mul(out=xs[:], in0=xc_tiles[j][:], scalar1=oma[:, 0:1])
+            xs_tiles[j] = xs
+
+        def y_mm(j):
+            acod, apl = acod_tiles[j]
+            py = ps_y.tile([P, NCH], F32, name="py", tag="y")
+            nc.tensor.matmul_mx(out=py[:], lhsT=wcod[:].bitcast(FP8X4), lhsT_scale=wpl[:],
+                                rhs=acod[:].bitcast(FP8X4), rhs_scale=apl[:], start=True, stop=True)
+            py_tiles[j] = py
+
+        def y_evac(j):
+            b, cols = out_cols(j)
+            ag = io_pool.tile([P, NCH], F32, name="ag", tag="ag", bufs=4)
+            nc.scalar.activation(out=ag[:], in_=py_tiles[j][:], func=ACT.Identity, bias=b32[:, 0:1], scale=1.0)
+            nc.sync.dma_start(out=o1_v[b][:, cols], in_=ag[:])
+            ag_tiles[j] = ag
+
+        def out_combine(j):
+            b, cols = out_cols(j)
+            o = io_pool.tile([P, NCH], F32, name="o", tag="o", bufs=4)
+            nc.vector.scalar_tensor_tensor(out=o[:], in0=ag_tiles[j][:], scalar=alpha[:, 0:1], in1=xs_tiles[j][:],
+                                           op0=ALU.mult, op1=ALU.add)
+            nc.sync.dma_start(out=o0_v[b][:, cols], in_=o[:])
+
+        def valid(j):
+            return 0 <= j < NSTEP
+
+        def second(j):
+            return valid(j) and (j // NCHUNK) % 2 == 1
+
+        nc.scalar.dma_start(out=praw[0][:], in_=ph_v[0])
+        for q in range(3):
+            load_theta(0, q)
+        nc.scalar.dma_start(out=wraw[:], in_=w_attn_g)
+        nc.scalar.dma_start(out=gam[:], in_=gamma.partition_broadcast(P))
+        nc.scalar.dma_start(out=braw[:], in_=b_attn_g.rearrange("(p o) -> p o", o=1))
+        nc.scalar.dma_start(out=praw[1][:], in_=ph_v[1])
+        for i in range(2):
+            load_g(i)
+        transpose_phi(0, 0)
+        evac_phi(0, 0)
+        transpose_theta(0, 0)
+        evac_theta(0, 0, False)
+        for t in range(4):
+            issue_s(0, t)
+        transpose_theta(0, 1)
+        evac_theta(0, 1, False)
+
+        setup = {}
+        for i4 in range(2, 8):
+            setup[i4 - 2] = [("theta", 0, i4)]
+        setup[6] = [("phi", 0, 1)]
+        setup[7] = [("w", 0, 0)]
+        setup[8] = [("phi", 1, 0)]
+        setup[9] = [("phi", 1, 1)]
+        for i4 in range(8):
+            setup[7 + i4] = setup.get(7 + i4, []) + [("theta", 1, i4)]
+        theta_loads = {0: (0, 3), 1: (1, 0), 3: (1, 1), 5: (1, 2), 7 + 1: (1, 3)}
+
+        for k in range(NSTEP + NCHUNK + 6):
+            j = k - NCHUNK
+            for what, sb, si in setup.get(k, []):
+                if what == "theta":
+                    transpose_theta(sb, si)
+                elif what == "phi":
+                    transpose_phi(sb, si)
+                else:
+                    transpose_w()
+            if k in theta_loads:
+                load_theta(theta_loads[k][0], theta_loads[k][1])
+            if second(j + 1):
+                x_load(j + 1)
+            for u in range(4):
+                if second(j - 2):
+                    a_mm(j - 2, u)
+                if k < NSTEP:
+                    red_exp(k, u)
+                if second(j - 2):
+                    a_evac(j - 2, u)
+                if k + 1 < NSTEP:
+                    issue_s(k + 1, u)
+                if u == 1 and second(j - 4):
+                    y_mm(j - 4)
+            if k < NSTEP and k % NCHUNK == NCHUNK - 1:
+                stats1(k // NCHUNK)
+            if valid(j) and j % NCHUNK == 0:
+                stats2(j // NCHUNK)
+            for what, sb, si in setup.get(k, []):
+                if what == "theta":
+                    evac_theta(sb, si, sb == 0)
+                elif what == "phi":
+                    evac_phi(sb, si)
+                else:
+                    evac_w()
+            if k == 3:
+                small_constants_s()
+            if k == 5:
+                small_constants_v()
+            if k == 8:
+                quant_w()
+            if k in (4, 6, 10, 12):
+                quant_g((4, 6, 10, 12).index(k))
+            if k in (0, 1, 5, 7):
+                regroup_g((0, 1, 5, 7).index(k))
+            if k in (0, 1):
+                load_g(k + 2)
+            if valid(j - 1):
+                quantise(j - 1)
+            if second(j - 3):
+                a_quant(j - 3)
+                x_scale(j - 3)
+            if second(j - 5):
+                out_combine(j - 5)
+            if valid(j + 1) and (j + 1) % NCHUNK != 0:
+                planes(j + 1, "v")
+            if valid(j):
+                normalise(j)
+            if second(j - 4):
+                y_evac(j - 4)
+            if valid(j + 1) and (j + 1) % NCHUNK != 0:
+                planes(j + 1, "GS")

@@ -33,7 +33,7 @@ XS_ENGINE = "G"
 
 
 def norm_engine(gi, c):
-    return "A" if (c == 0 or gi == 1) else ("SSSv" if gi != 3 else "A")
+    return "A" if c == 0 else ("GGSS" if gi in (0,2) else ("GGSv" if gi == 1 else "Svvv"))
 
 
 def tile_selfattention3d_pa_t_kernel(tc, theta, phi, g, x, w_attn_g, b_attn_g, gamma, out_0, out_1):

@@ -25,9 +25,10 @@ NSTEP = 4 * NCHUNK
 
 FLOPS = 2 * B * (NQ * NK * C1 + NQ * NK * C2 + CH * C2 * NQ)
 
-MANUAL = True
+MANUAL = False
 E_BUFS = 10
 S_BANKS = 5
+LAG = 8
 G_REGROUP = "G"
 XS_ENGINE = "G"
 
@@ -319,7 +320,7 @@ def tile_selfattention3d_pa_t_kernel(tc, theta, phi, g, x, w_attn_g, b_attn_g, g
 
         def x_scale(j):
             xs = io_pool.tile([P, NCH], F32, name="xs", tag="xs", bufs=3)
-            if XS_ENGINE == "G":
+            if XS_ENGINE == "G" or (XS_ENGINE == "M" and j < 2 * NCHUNK):
                 nc.gpsimd.tensor_scalar(out=xs[:], in0=xc_tiles[j][:], scalar1=oma[:, 0:1], scalar2=0.0, op0=ALU.mult,
                                         op1=ALU.add)
             else:
@@ -382,8 +383,8 @@ def tile_selfattention3d_pa_t_kernel(tc, theta, phi, g, x, w_attn_g, b_attn_g, g
             setup[7 + i4] = setup.get(7 + i4, []) + [("theta", 1, i4)]
         theta_loads = {0: (0, 3), 1: (1, 0), 3: (1, 1), 5: (1, 2), 7 + 1: (1, 3)}
 
-        for k in range(NSTEP + NCHUNK + 6):
-            j = k - NCHUNK
+        for k in range(NSTEP + LAG + 6):
+            j = k - LAG
             for what, sb, si in setup.get(k, []):
                 if what == "theta":
                     transpose_theta(sb, si)
@@ -408,8 +409,8 @@ def tile_selfattention3d_pa_t_kernel(tc, theta, phi, g, x, w_attn_g, b_attn_g, g
                     y_mm(j - 4)
             if k < NSTEP and k % NCHUNK == NCHUNK - 1:
                 stats1(k // NCHUNK)
-            if valid(j) and j % NCHUNK == 0:
-                stats2(j // NCHUNK)
+            if k >= NCHUNK and k % NCHUNK == 0 and k <= NSTEP:
+                stats2(k // NCHUNK - 1)
             for what, sb, si in setup.get(k, []):
                 if what == "theta":
                     evac_theta(sb, si, sb == 0)
@@ -436,11 +437,11 @@ def tile_selfattention3d_pa_t_kernel(tc, theta, phi, g, x, w_attn_g, b_attn_g, g
                 x_scale(j - 3)
             if second(j - 5):
                 out_combine(j - 5)
-            if valid(j + 1) and (j + 1) % NCHUNK != 0:
+            if valid(j + 1) and (LAG > NCHUNK or (j + 1) % NCHUNK != 0):
                 planes(j + 1, "v")
             if valid(j):
                 normalise(j)
             if second(j - 4):
                 y_evac(j - 4)
-            if valid(j + 1) and (j + 1) % NCHUNK != 0:
+            if valid(j + 1) and (LAG > NCHUNK or (j + 1) % NCHUNK != 0):
                 planes(j + 1, "GS")

@@ -43,7 +43,7 @@ def tile_selfattention3d_pa_t_kernel(tc, theta, phi, g, x, w_attn_g, b_attn_g, g
         if MANUAL:
             ctx.enter_context(tc.manual_schedule())
         const = ctx.enter_context(tc.tile_pool(name="const", bufs=1))
-        raw = ctx.enter_context(tc.tile_pool(name="raw", bufs=3))
+        raw = ctx.enter_context(tc.tile_pool(name="raw", bufs=8))
         graw_pool = ctx.enter_context(tc.tile_pool(name="graw", bufs=2))
         gg_pool = ctx.enter_context(tc.tile_pool(name="gg", bufs=2))
         e_pool = ctx.enter_context(tc.tile_pool(name="e", bufs=E_BUFS))
@@ -87,10 +87,10 @@ def tile_selfattention3d_pa_t_kernel(tc, theta, phi, g, x, w_attn_g, b_attn_g, g
         graws = {}
         ggs = {}
 
-        def load_theta(b, q):
-            traw = raw.tile([P, 8, C1], BF16, name="traw", tag="traw")
-            nc.sync.dma_start(out=traw[:], in_=th_v[b][:, 8 * q:8 * q + 8, :])
-            traws[(b, q)] = traw
+        def load_theta(b, c):
+            traw = raw.tile([P, 4, C1], BF16, name="traw", tag="traw")
+            nc.sync.dma_start(out=traw[:], in_=th_v[b][:, 4 * c:4 * c + 4, :])
+            traws[(b, c)] = traw
 
         def load_g(i):
             gr = graw_pool.tile([P, 4, C2], BF16, name="gr", tag="gr")
@@ -109,11 +109,10 @@ def tile_selfattention3d_pa_t_kernel(tc, theta, phi, g, x, w_attn_g, b_attn_g, g
             nc.vector.tensor_scalar_mul(out=nphiT[b][:, 4 * h:4 * h + 4, :], in0=pts[("phi", b, h)][:], scalar1=-1.0)
 
         def transpose_theta(b, i4):
-            q, h = divmod(i4, 2)
-            traw = traws[(b, q)]
+            traw = traws[(b, i4)]
             pt = ps_a.tile([P, 4, P], BF16, name="pt", tag="a")
             for i in range(4):
-                nc.tensor.transpose(pt[:, i, :], traw[:, 4 * h + i, :], ident[:])
+                nc.tensor.transpose(pt[:, i, :], traw[:, i, :], ident[:])
             pts[("theta", b, i4)] = pt
 
         def evac_theta(b, i4, use_vector):
@@ -279,7 +278,10 @@ def tile_selfattention3d_pa_t_kernel(tc, theta, phi, g, x, w_attn_g, b_attn_g, g
         def a_mm(j, sub):
             b = j // (2 * NCHUNK)
             ops = [cod_tiles[j - NCHUNK], cod_tiles[j]]
-            pa = ps_a.tile([P, 4, P], F32, name="pa", tag="a")
+            if b == 0:
+                pa = ps_a.tile([P, 4, P], F32, name="pa", tag="a")
+            else:
+                pa = ps_s.tile([P, 4, P], F32, name="pa", tag="s")
             cols = slice(sub * P, (sub + 1) * P)
             for jj in range(4):
                 mcols = slice(jj * P, (jj + 1) * P)
@@ -354,13 +356,16 @@ def tile_selfattention3d_pa_t_kernel(tc, theta, phi, g, x, w_attn_g, b_attn_g, g
         def second(j):
             return valid(j) and (j // NCHUNK) % 2 == 1
 
-        nc.scalar.dma_start(out=praw[0][:], in_=ph_v[0])
-        for q in range(3):
-            load_theta(0, q)
-        nc.scalar.dma_start(out=wraw[:], in_=w_attn_g)
-        nc.scalar.dma_start(out=gam[:], in_=gamma.partition_broadcast(P))
-        nc.scalar.dma_start(out=braw[:], in_=b_attn_g.rearrange("(p o) -> p o", o=1))
-        nc.scalar.dma_start(out=praw[1][:], in_=ph_v[1])
+        nc.sync.dma_start(out=praw[0][:, 0, :, :], in_=ph_v[0][:, 0, :, :])
+        load_theta(0, 0)
+        load_theta(0, 1)
+        nc.gpsimd.dma_start(out=gam[:], in_=gamma.partition_broadcast(P))
+        nc.gpsimd.dma_start(out=braw[:], in_=b_attn_g.rearrange("(p o) -> p o", o=1))
+        for c in range(2, NCHUNK):
+            load_theta(0, c)
+        nc.sync.dma_start(out=praw[0][:, 1, :, :], in_=ph_v[0][:, 1, :, :])
+        nc.sync.dma_start(out=wraw[:], in_=w_attn_g)
+        nc.sync.dma_start(out=praw[1][:], in_=ph_v[1])
         for i in range(2):
             load_g(i)
         transpose_phi(0, 0)
@@ -381,7 +386,6 @@ def tile_selfattention3d_pa_t_kernel(tc, theta, phi, g, x, w_attn_g, b_attn_g, g
         setup[9] = [("phi", 1, 1)]
         for i4 in range(8):
             setup[7 + i4] = setup.get(7 + i4, []) + [("theta", 1, i4)]
-        theta_loads = {0: (0, 3), 1: (1, 0), 3: (1, 1), 5: (1, 2), 7 + 1: (1, 3)}
 
         for k in range(NSTEP + LAG + 6):
             j = k - LAG
@@ -392,8 +396,8 @@ def tile_selfattention3d_pa_t_kernel(tc, theta, phi, g, x, w_attn_g, b_attn_g, g
                     transpose_phi(sb, si)
                 else:
                     transpose_w()
-            if k in theta_loads:
-                load_theta(theta_loads[k][0], theta_loads[k][1])
+            if k < NCHUNK:
+                load_theta(1, k)
             if second(j + 1):
                 x_load(j + 1)
             for u in range(4):

@@ -25,7 +25,7 @@ NSTEP = 4 * NCHUNK
 
 FLOPS = 2 * B * (NQ * NK * C1 + NQ * NK * C2 + CH * C2 * NQ)
 
-MANUAL = False
+MANUAL = True
 E_BUFS = 10
 S_BANKS = 5
 LAG = 8
@@ -81,7 +81,6 @@ def tile_selfattention3d_pa_t_kernel(tc, theta, phi, g, x, w_attn_g, b_attn_g, g
         braw = const.tile([P, 1], BF16, name="braw")
         alpha = const.tile([P, 1], F32, name="alpha")
         oma = const.tile([P, 1], F32, name="oma")
-        b32 = const.tile([P, 1], F32, name="b32")
 
         traws = {}
         graws = {}
@@ -147,7 +146,6 @@ def tile_selfattention3d_pa_t_kernel(tc, theta, phi, g, x, w_attn_g, b_attn_g, g
             nc.vector.tensor_scalar_add(out=den[:], in0=eg[:], scalar1=1.0)
             nc.vector.reciprocal(out=alpha[:], in_=den[:])
             nc.vector.tensor_scalar(out=oma[:], in0=alpha[:], scalar1=-1.0, scalar2=1.0, op0=ALU.mult, op1=ALU.add)
-            nc.vector.tensor_copy(out=b32[:], in_=braw[:])
 
         wgs = {}
 
@@ -297,11 +295,18 @@ def tile_selfattention3d_pa_t_kernel(tc, theta, phi, g, x, w_attn_g, b_attn_g, g
                     )
             pa_tiles[(j, sub)] = pa
 
+        def on_vector(j, sub):
+            return j >= NSTEP - 0 and sub >= 2
+
         def a_evac(j, sub):
             if sub == 0:
                 agrp_tiles[j] = a_pool.tile([P, NCH, 4], BF16, name="agrp", tag="agrp", align_bytes=64)
-            nc.scalar.copy(out=agrp_tiles[j][:, sub * P:(sub + 1) * P, :],
-                           in_=pa_tiles[(j, sub)][:].rearrange("p j n -> p n j"))
+            if on_vector(j, sub):
+                nc.vector.tensor_copy(out=agrp_tiles[j][:, sub * P:(sub + 1) * P, :],
+                                      in_=pa_tiles[(j, sub)][:].rearrange("p j n -> p n j"))
+            else:
+                nc.scalar.copy(out=agrp_tiles[j][:, sub * P:(sub + 1) * P, :],
+                               in_=pa_tiles[(j, sub)][:].rearrange("p j n -> p n j"))
 
         def a_quant(j):
             acod = a_pool.tile([P, NCH], U32, name="acod", tag="acod", align_bytes=64)
@@ -339,7 +344,7 @@ def tile_selfattention3d_pa_t_kernel(tc, theta, phi, g, x, w_attn_g, b_attn_g, g
         def y_evac(j):
             b, cols = out_cols(j)
             ag = io_pool.tile([P, NCH], F32, name="ag", tag="ag", bufs=4)
-            nc.scalar.activation(out=ag[:], in_=py_tiles[j][:], func=ACT.Identity, bias=b32[:, 0:1], scale=1.0)
+            nc.scalar.activation(out=ag[:], in_=py_tiles[j][:], func=ACT.Identity, bias=braw[:, 0:1], scale=1.0)
             nc.sync.dma_start(out=o1_v[b][:, cols], in_=ag[:])
             ag_tiles[j] = ag
 
@@ -356,11 +361,11 @@ def tile_selfattention3d_pa_t_kernel(tc, theta, phi, g, x, w_attn_g, b_attn_g, g
         def second(j):
             return valid(j) and (j // NCHUNK) % 2 == 1
 
+        nc.scalar.dma_start(out=gam[:], in_=gamma.partition_broadcast(P))
+        nc.scalar.dma_start(out=braw[:], in_=b_attn_g.rearrange("(p o) -> p o", o=1))
         nc.sync.dma_start(out=praw[0][:, 0, :, :], in_=ph_v[0][:, 0, :, :])
         load_theta(0, 0)
         load_theta(0, 1)
-        nc.gpsimd.dma_start(out=gam[:], in_=gamma.partition_broadcast(P))
-        nc.gpsimd.dma_start(out=braw[:], in_=b_attn_g.rearrange("(p o) -> p o", o=1))
         for c in range(2, NCHUNK):
             load_theta(0, c)
         nc.sync.dma_start(out=praw[0][:, 1, :, :], in_=ph_v[0][:, 1, :, :])
@@ -405,7 +410,7 @@ def tile_selfattention3d_pa_t_kernel(tc, theta, phi, g, x, w_attn_g, b_attn_g, g
                     a_mm(j - 2, u)
                 if k < NSTEP:
                     red_exp(k, u)
-                if second(j - 2):
+                if second(j - 2) and not on_vector(j - 2, u):
                     a_evac(j - 2, u)
                 if k + 1 < NSTEP:
                     issue_s(k + 1, u)
@@ -441,8 +446,13 @@ def tile_selfattention3d_pa_t_kernel(tc, theta, phi, g, x, w_attn_g, b_attn_g, g
                 x_scale(j - 3)
             if second(j - 5):
                 out_combine(j - 5)
+            for u in range(4):
+                if second(j - 2) and on_vector(j - 2, u):
+                    a_evac(j - 2, u)
             if valid(j + 1) and (LAG > NCHUNK or (j + 1) % NCHUNK != 0):
                 planes(j + 1, "v")
+            if LAG == NCHUNK and valid(j) and j % NCHUNK == 0:
+                planes(j, "vGS")
             if valid(j):
                 normalise(j)
             if second(j - 4):

@@ -25,7 +25,7 @@ NSTEP = 4 * NCHUNK
 
 FLOPS = 2 * B * (NQ * NK * C1 + NQ * NK * C2 + CH * C2 * NQ)
 
-MANUAL = True
+MANUAL = False
 E_BUFS = 10
 S_BANKS = 5
 LAG = 8
@@ -34,7 +34,7 @@ XS_ENGINE = "G"
 
 
 def norm_engine(gi, c):
-    return "A" if c == 0 else ("GGSS" if gi in (0,2) else ("GGSv" if gi == 1 else "Svvv"))
+    return "A" if c == 0 else ("GGGS" if gi in (0,2) else ("GGGv" if gi == 1 else "Svvv"))
 
 
 def tile_selfattention3d_pa_t_kernel(tc, theta, phi, g, x, w_attn_g, b_attn_g, gamma, out_0, out_1):
@@ -81,6 +81,7 @@ def tile_selfattention3d_pa_t_kernel(tc, theta, phi, g, x, w_attn_g, b_attn_g, g
         braw = const.tile([P, 1], BF16, name="braw")
         alpha = const.tile([P, 1], F32, name="alpha")
         oma = const.tile([P, 1], F32, name="oma")
+        b32 = const.tile([P, 1], F32, name="b32")
 
         traws = {}
         graws = {}
@@ -146,6 +147,7 @@ def tile_selfattention3d_pa_t_kernel(tc, theta, phi, g, x, w_attn_g, b_attn_g, g
             nc.vector.tensor_scalar_add(out=den[:], in0=eg[:], scalar1=1.0)
             nc.vector.reciprocal(out=alpha[:], in_=den[:])
             nc.vector.tensor_scalar(out=oma[:], in0=alpha[:], scalar1=-1.0, scalar2=1.0, op0=ALU.mult, op1=ALU.add)
+            nc.vector.tensor_copy(out=b32[:], in_=braw[:])
 
         wgs = {}
 
@@ -344,7 +346,7 @@ def tile_selfattention3d_pa_t_kernel(tc, theta, phi, g, x, w_attn_g, b_attn_g, g
         def y_evac(j):
             b, cols = out_cols(j)
             ag = io_pool.tile([P, NCH], F32, name="ag", tag="ag", bufs=4)
-            nc.scalar.activation(out=ag[:], in_=py_tiles[j][:], func=ACT.Identity, bias=braw[:, 0:1], scale=1.0)
+            nc.scalar.activation(out=ag[:], in_=py_tiles[j][:], func=ACT.Identity, bias=b32[:, 0:1], scale=1.0)
             nc.sync.dma_start(out=o1_v[b][:, cols], in_=ag[:])
             ag_tiles[j] = ag
 
@@ -361,11 +363,11 @@ def tile_selfattention3d_pa_t_kernel(tc, theta, phi, g, x, w_attn_g, b_attn_g, g
         def second(j):
             return valid(j) and (j // NCHUNK) % 2 == 1
 
-        nc.scalar.dma_start(out=gam[:], in_=gamma.partition_broadcast(P))
-        nc.scalar.dma_start(out=braw[:], in_=b_attn_g.rearrange("(p o) -> p o", o=1))
         nc.sync.dma_start(out=praw[0][:, 0, :, :], in_=ph_v[0][:, 0, :, :])
         load_theta(0, 0)
         load_theta(0, 1)
+        nc.gpsimd.dma_start(out=gam[:], in_=gamma.partition_broadcast(P))
+        nc.gpsimd.dma_start(out=braw[:], in_=b_attn_g.rearrange("(p o) -> p o", o=1))
         for c in range(2, NCHUNK):
             load_theta(0, c)
         nc.sync.dma_start(out=praw[0][:, 1, :, :], in_=ph_v[0][:, 1, :, :])

@@ -30,11 +30,11 @@ E_BUFS = 10
 S_BANKS = 5
 LAG = 8
 G_REGROUP = "G"
-XS_ENGINE = "G"
+XS_ENGINE = "M"
 
 
 def norm_engine(gi, c):
-    return "A" if c == 0 else ("GGGS" if gi in (0,2) else ("GGGv" if gi == 1 else "Svvv"))
+    return "A" if c == 0 else ("GGSS" if gi in (0,2) else ("GGSv" if gi == 1 else "Svvv"))
 
 
 def tile_selfattention3d_pa_t_kernel(tc, theta, phi, g, x, w_attn_g, b_attn_g, gamma, out_0, out_1):

@@ -25,11 +25,10 @@ NSTEP = 4 * NCHUNK
 
 FLOPS = 2 * B * (NQ * NK * C1 + NQ * NK * C2 + CH * C2 * NQ)
 
-MANUAL = False
+PINNED = 15
 E_BUFS = 10
 S_BANKS = 5
 LAG = 8
-G_REGROUP = "G"
 XS_ENGINE = "M"
 
 
@@ -40,8 +39,6 @@ def norm_engine(gi, c):
 def tile_selfattention3d_pa_t_kernel(tc, theta, phi, g, x, w_attn_g, b_attn_g, gamma, out_0, out_1):
     nc = tc.nc
     with ExitStack() as ctx:
-        if MANUAL:
-            ctx.enter_context(tc.manual_schedule())
         const = ctx.enter_context(tc.tile_pool(name="const", bufs=1))
         raw = ctx.enter_context(tc.tile_pool(name="raw", bufs=8))
         graw_pool = ctx.enter_context(tc.tile_pool(name="graw", bufs=2))
@@ -53,7 +50,7 @@ def tile_selfattention3d_pa_t_kernel(tc, theta, phi, g, x, w_attn_g, b_attn_g, g
         cod0_pool = ctx.enter_context(tc.tile_pool(name="cod0", bufs=8))
         cod1_pool = ctx.enter_context(tc.tile_pool(name="cod1", bufs=3))
         a_pool = ctx.enter_context(tc.tile_pool(name="a", bufs=2))
-        x_pool = ctx.enter_context(tc.tile_pool(name="x", bufs=6))
+        x_pool = ctx.enter_context(tc.tile_pool(name="x", bufs=8))
         io_pool = ctx.enter_context(tc.tile_pool(name="io", bufs=2))
         ps_s = ctx.enter_context(tc.psum_pool(name="ps_s", bufs=S_BANKS))
         ps_a = ctx.enter_context(tc.psum_pool(name="ps_a", bufs=2))
@@ -125,12 +122,8 @@ def tile_selfattention3d_pa_t_kernel(tc, theta, phi, g, x, w_attn_g, b_attn_g, g
 
         def regroup_g(i):
             gg = gg_pool.tile([P, C2, 4], BF16, name="gg", tag="gg", align_bytes=64)
-            dst = gg[:].rearrange("p (c i) t -> p c t i", i=4)
-            srcv = graws[i][:].rearrange("p t (c i) -> p c t i", i=4)
-            if G_REGROUP == "G":
-                nc.gpsimd.tensor_scalar(out=dst, in0=srcv, scalar1=1.0, scalar2=0.0, op0=ALU.mult, op1=ALU.add)
-            else:
-                nc.vector.tensor_copy(out=dst, in_=srcv)
+            nc.gpsimd.tensor_scalar(out=gg[:], in0=graws[i][:].rearrange("p t c -> p c t"), scalar1=1.0, scalar2=0.0,
+                                    op0=ALU.mult, op1=ALU.add)
             ggs[i] = gg
 
         def quant_g(i):
@@ -249,16 +242,20 @@ def tile_selfattention3d_pa_t_kernel(tc, theta, phi, g, x, w_attn_g, b_attn_g, g
                 else:
                     nc.vector.tensor_scalar_mul(out=pl[:, t, :], in0=e[:, t, :], scalar1=sc[:, t, c:c + 1])
 
+        def spans(j):
+            return ((0, NCH // 2), (NCH // 2, NCH)) if j == NSTEP - NCHUNK else ((0, NCH),)
+
         def normalise(j):
             gi, c = divmod(j, NCHUNK)
             grp = grp_pool.tile([P, NCH, 4], BF16, name="grp", tag="grp", align_bytes=64)
             if norm_engine(gi, c) == "A":
-                nc.vector.tensor_tensor(
-                    out=grp[:].rearrange("p (c i) t -> p c t i", i=4),
-                    in0=e_tiles[j][:].rearrange("p t (c i) -> p c t i", i=4),
-                    in1=sc_tiles[gi][:, :, c:c + 1].unsqueeze(1).to_broadcast([P, NCH // 4, 4, 4]),
-                    op=ALU.mult,
-                )
+                for n0, n1 in spans(j):
+                    nc.vector.tensor_tensor(
+                        out=grp[:, n0:n1, :].rearrange("p (c i) t -> p c t i", i=4),
+                        in0=e_tiles[j][:, :, n0:n1].rearrange("p t (c i) -> p c t i", i=4),
+                        in1=sc_tiles[gi][:, :, c:c + 1].unsqueeze(1).to_broadcast([P, (n1 - n0) // 4, 4, 4]),
+                        op=ALU.mult,
+                    )
             else:
                 nc.vector.tensor_copy(
                     out=grp[:].rearrange("p (c i) t -> p c t i", i=4),
@@ -271,8 +268,9 @@ def tile_selfattention3d_pa_t_kernel(tc, theta, phi, g, x, w_attn_g, b_attn_g, g
             pool = cod0_pool if gi % 2 == 0 else cod1_pool
             cod = pool.tile([P, NCH], U32, name="cod", tag="cod", align_bytes=64)
             pln = pool.tile([P, NCH], U8, name="pln", tag="pln", align_bytes=64)
-            nc.vector.quantize_mx(out=cod[:].bitcast(FP8X4), scales=pln[:],
-                                  in_=grp_tiles[j][:].rearrange("p n t -> p (n t)"))
+            for n0, n1 in spans(j):
+                nc.vector.quantize_mx(out=cod[:, n0:n1].bitcast(FP8X4), scales=pln[:, n0:n1],
+                                      in_=grp_tiles[j][:, n0:n1, :].rearrange("p n t -> p (n t)"))
             cod_tiles[j] = (cod, pln)
 
         def a_mm(j, sub):
@@ -345,7 +343,7 @@ def tile_selfattention3d_pa_t_kernel(tc, theta, phi, g, x, w_attn_g, b_attn_g, g
 
         def y_evac(j):
             b, cols = out_cols(j)
-            ag = io_pool.tile([P, NCH], F32, name="ag", tag="ag", bufs=4)
+            ag = io_pool.tile([P, NCH], F32, name="ag", tag="ag", bufs=6)
             nc.scalar.activation(out=ag[:], in_=py_tiles[j][:], func=ACT.Identity, bias=b32[:, 0:1], scale=1.0)
             nc.sync.dma_start(out=o1_v[b][:, cols], in_=ag[:])
             ag_tiles[j] = ag
@@ -363,27 +361,6 @@ def tile_selfattention3d_pa_t_kernel(tc, theta, phi, g, x, w_attn_g, b_attn_g, g
         def second(j):
             return valid(j) and (j // NCHUNK) % 2 == 1
 
-        nc.sync.dma_start(out=praw[0][:, 0, :, :], in_=ph_v[0][:, 0, :, :])
-        load_theta(0, 0)
-        load_theta(0, 1)
-        nc.gpsimd.dma_start(out=gam[:], in_=gamma.partition_broadcast(P))
-        nc.gpsimd.dma_start(out=braw[:], in_=b_attn_g.rearrange("(p o) -> p o", o=1))
-        for c in range(2, NCHUNK):
-            load_theta(0, c)
-        nc.sync.dma_start(out=praw[0][:, 1, :, :], in_=ph_v[0][:, 1, :, :])
-        nc.sync.dma_start(out=wraw[:], in_=w_attn_g)
-        nc.sync.dma_start(out=praw[1][:], in_=ph_v[1])
-        for i in range(2):
-            load_g(i)
-        transpose_phi(0, 0)
-        evac_phi(0, 0)
-        transpose_theta(0, 0)
-        evac_theta(0, 0, False)
-        for t in range(4):
-            issue_s(0, t)
-        transpose_theta(0, 1)
-        evac_theta(0, 1, False)
-
         setup = {}
         for i4 in range(2, 8):
             setup[i4 - 2] = [("theta", 0, i4)]
@@ -394,7 +371,7 @@ def tile_selfattention3d_pa_t_kernel(tc, theta, phi, g, x, w_attn_g, b_attn_g, g
         for i4 in range(8):
             setup[7 + i4] = setup.get(7 + i4, []) + [("theta", 1, i4)]
 
-        for k in range(NSTEP + LAG + 6):
+        def step(k):
             j = k - LAG
             for what, sb, si in setup.get(k, []):
                 if what == "theta":
@@ -441,13 +418,17 @@ def tile_selfattention3d_pa_t_kernel(tc, theta, phi, g, x, w_attn_g, b_attn_g, g
                 regroup_g((0, 1, 5, 7).index(k))
             if k in (0, 1):
                 load_g(k + 2)
-            if valid(j - 1):
+            if valid(j - 1) and j - 1 != NSTEP - NCHUNK:
                 quantise(j - 1)
             if second(j - 3):
                 a_quant(j - 3)
-                x_scale(j - 3)
-            if second(j - 5):
+                if j - 3 < 2 * NCHUNK:
+                    x_scale(j - 3)
+            if second(j - 5) and j - 5 < 2 * NCHUNK:
                 out_combine(j - 5)
+            if second(j - 7) and j - 7 >= 2 * NCHUNK:
+                x_scale(j - 7)
+                out_combine(j - 7)
             for u in range(4):
                 if second(j - 2) and on_vector(j - 2, u):
                     a_evac(j - 2, u)
@@ -457,7 +438,36 @@ def tile_selfattention3d_pa_t_kernel(tc, theta, phi, g, x, w_attn_g, b_attn_g, g
                 planes(j, "vGS")
             if valid(j):
                 normalise(j)
+            if j == NSTEP - NCHUNK:
+                quantise(j)
             if second(j - 4):
                 y_evac(j - 4)
             if valid(j + 1) and (LAG > NCHUNK or (j + 1) % NCHUNK != 0):
                 planes(j + 1, "GS")
+
+        with tc.manual_schedule():
+            nc.sync.dma_start(out=praw[0][:, 0, :, :], in_=ph_v[0][:, 0, :, :])
+            load_theta(0, 0)
+            load_theta(0, 1)
+            nc.gpsimd.dma_start(out=gam[:], in_=gamma.partition_broadcast(P))
+            nc.gpsimd.dma_start(out=braw[:], in_=b_attn_g.rearrange("(p o) -> p o", o=1))
+            for c in range(2, NCHUNK):
+                load_theta(0, c)
+            nc.sync.dma_start(out=praw[0][:, 1, :, :], in_=ph_v[0][:, 1, :, :])
+            nc.sync.dma_start(out=wraw[:], in_=w_attn_g)
+            nc.sync.dma_start(out=praw[1][:], in_=ph_v[1])
+            for i in range(2):
+                load_g(i)
+            transpose_phi(0, 0)
+            evac_phi(0, 0)
+            transpose_theta(0, 0)
+            evac_theta(0, 0, False)
+            for t in range(4):
+                issue_s(0, t)
+            transpose_theta(0, 1)
+            evac_theta(0, 1, False)
+
+            for k in range(PINNED):
+                step(k)
+        for k in range(PINNED, NSTEP + LAG + 8):
+            step(k)

from contextlib import ExitStack

import concourse.masks as masks
import concourse.mybir as mybir

F32 = mybir.dt.float32
BF16 = mybir.dt.bfloat16
U32 = mybir.dt.uint32
U8 = mybir.dt.uint8
FP8X4 = mybir.dt.float8_e4m3fn_x4
ALU = mybir.AluOpType
ACT = mybir.ActivationFunctionType
AX = mybir.AxisListType

P = 128
B = 2
NQ = 4096
NK = 1024
C1 = 128
C2 = 512
CH = 128
NCH = 512
NCHUNK = NQ // NCH
NSTEP = 4 * NCHUNK

FLOPS = 2 * B * (NQ * NK * C1 + NQ * NK * C2 + CH * C2 * NQ)

PINNED = 15
E_BUFS = 10
S_BANKS = 5
LAG = 8
XS_ENGINE = "M"


def norm_engine(gi, c):
    return "A" if c == 0 else ("GGSS" if gi in (0,2) else ("GGSv" if gi == 1 else "Svvv"))


def tile_selfattention3d_pa_t_kernel(tc, theta, phi, g, x, w_attn_g, b_attn_g, gamma, out_0, out_1):
    nc = tc.nc
    with ExitStack() as ctx:
        const = ctx.enter_context(tc.tile_pool(name="const", bufs=1))
        raw = ctx.enter_context(tc.tile_pool(name="raw", bufs=8))
        graw_pool = ctx.enter_context(tc.tile_pool(name="graw", bufs=2))
        gg_pool = ctx.enter_context(tc.tile_pool(name="gg", bufs=2))
        e_pool = ctx.enter_context(tc.tile_pool(name="e", bufs=E_BUFS))
        st_pool = ctx.enter_context(tc.tile_pool(name="st", bufs=2))
        pl_pool = ctx.enter_context(tc.tile_pool(name="pl", bufs=2))
        grp_pool = ctx.enter_context(tc.tile_pool(name="grp", bufs=2))
        cod0_pool = ctx.enter_context(tc.tile_pool(name="cod0", bufs=8))
        cod1_pool = ctx.enter_context(tc.tile_pool(name="cod1", bufs=3))
        a_pool = ctx.enter_context(tc.tile_pool(name="a", bufs=2))
        x_pool = ctx.enter_context(tc.tile_pool(name="x", bufs=8))
        io_pool = ctx.enter_context(tc.tile_pool(name="io", bufs=2))
        ps_s = ctx.enter_context(tc.psum_pool(name="ps_s", bufs=S_BANKS))
        ps_a = ctx.enter_context(tc.psum_pool(name="ps_a", bufs=2))
        ps_y = ctx.enter_context(tc.psum_pool(name="ps_y", bufs=1))

        th_v = [theta[b].rearrange("(r p) c -> p r c", p=P) for b in range(B)]
        ph_v = [phi[b].rearrange("(g p t) c -> p g t c", g=2, p=P, t=4) for b in range(B)]
        g_v = [g[b].rearrange("(g p j) c -> p g j c", g=2, p=P, j=4) for b in range(B)]
        x_v = [x[b].rearrange("c f w h -> c (f w h)") for b in range(B)]
        o0_v = [out_0[b].rearrange("c f w h -> c (f w h)") for b in range(B)]
        o1_v = [out_1[b].rearrange("c f w h -> c (f w h)") for b in range(B)]

        ident = const.tile([P, P], BF16, name="ident")
        masks.make_identity(nc, ident[:])

        thetaT = [const.tile([P, NQ], BF16, name="thetaT%d" % b) for b in range(B)]
        nphiT = [const.tile([P, 8, P], BF16, name="nphiT%d" % b) for b in range(B)]
        gcod = [const.tile([P, C2], U32, name="gcod%d" % i, align_bytes=64) for i in range(4)]
        gpl = [const.tile([P, C2], U8, name="gpl%d" % i, align_bytes=64) for i in range(4)]
        wcod = const.tile([P, CH], U32, name="wcod", align_bytes=64)
        wpl = const.tile([P, CH], U8, name="wpl", align_bytes=64)
        praw = [const.tile([P, 2, 4, C1], BF16, name="praw%d" % b) for b in range(B)]
        wraw = const.tile([P, C2], BF16, name="wraw")
        gam = const.tile([P, 1], BF16, name="gam")
        braw = const.tile([P, 1], BF16, name="braw")
        alpha = const.tile([P, 1], F32, name="alpha")
        oma = const.tile([P, 1], F32, name="oma")
        b32 = const.tile([P, 1], F32, name="b32")

        traws = {}
        graws = {}
        ggs = {}

        def load_theta(b, c):
            traw = raw.tile([P, 4, C1], BF16, name="traw", tag="traw")
            nc.sync.dma_start(out=traw[:], in_=th_v[b][:, 4 * c:4 * c + 4, :])
            traws[(b, c)] = traw

        def load_g(i):
            gr = graw_pool.tile([P, 4, C2], BF16, name="gr", tag="gr")
            nc.sync.dma_start(out=gr[:], in_=g_v[i // 2][:, i % 2, :, :])
            graws[i] = gr

        pts = {}

        def transpose_phi(b, h):
            pt = ps_a.tile([P, 4, P], BF16, name="pt", tag="a")
            for i in range(4):
                nc.tensor.transpose(pt[:, i, :], praw[b][:, h, i, :], ident[:])
            pts[("phi", b, h)] = pt

        def evac_phi(b, h):
            nc.vector.tensor_scalar_mul(out=nphiT[b][:, 4 * h:4 * h + 4, :], in0=pts[("phi", b, h)][:], scalar1=-1.0)

        def transpose_theta(b, i4):
            traw = traws[(b, i4)]
            pt = ps_a.tile([P, 4, P], BF16, name="pt", tag="a")
            for i in range(4):
                nc.tensor.transpose(pt[:, i, :], traw[:, i, :], ident[:])
            pts[("theta", b, i4)] = pt

        def evac_theta(b, i4, use_vector):
            pt = pts[("theta", b, i4)]
            dst = thetaT[b][:, i4 * NCH:(i4 + 1) * NCH]
            if use_vector:
                nc.vector.tensor_copy(out=dst, in_=pt[:].rearrange("p i n -> p (i n)"))
            else:
                nc.scalar.copy(out=dst, in_=pt[:].rearrange("p i n -> p (i n)"))

        def regroup_g(i):
            gg = gg_pool.tile([P, C2, 4], BF16, name="gg", tag="gg", align_bytes=64)
            nc.gpsimd.tensor_scalar(out=gg[:], in0=graws[i][:].rearrange("p t c -> p c t"), scalar1=1.0, scalar2=0.0,
                                    op0=ALU.mult, op1=ALU.add)
            ggs[i] = gg

        def quant_g(i):
            nc.vector.quantize_mx(out=gcod[i][:].bitcast(FP8X4), scales=gpl[i][:],
                                  in_=ggs[i][:].rearrange("p c t -> p (c t)"))

        eg = const.tile([P, 1], F32, name="eg")

        def small_constants_s():
            nc.scalar.activation(out=eg[:], in_=gam[:], func=ACT.Exp, scale=-1.0)

        def small_constants_v():
            den = const.tile([P, 1], F32, name="den")
            nc.vector.tensor_scalar_add(out=den[:], in0=eg[:], scalar1=1.0)
            nc.vector.reciprocal(out=alpha[:], in_=den[:])
            nc.vector.tensor_scalar(out=oma[:], in0=alpha[:], scalar1=-1.0, scalar2=1.0, op0=ALU.mult, op1=ALU.add)
            nc.vector.tensor_copy(out=b32[:], in_=braw[:])

        wgs = {}

        def transpose_w():
            wt = ps_y.tile([P, 4, P], BF16, name="wt", tag="y")
            for j in range(4):
                nc.tensor.transpose(wt[:, j, :], wraw[:, j * P:(j + 1) * P], ident[:])
            wgs[1] = wt

        def evac_w():
            wg = const.tile([P, CH, 4], BF16, name="wg", align_bytes=64)
            nc.vector.tensor_copy(out=wg[:], in_=wgs[1][:].rearrange("p j c -> p c j"))
            wgs[0] = wg

        def quant_w():
            nc.vector.quantize_mx(out=wcod[:].bitcast(FP8X4), scales=wpl[:],
                                  in_=wgs[0][:].rearrange("p c j -> p (c j)"))

        ps_tiles = {}
        e_tiles = {}
        nm_tiles = {}
        sm_tiles = {}
        f_tiles = {}
        sc_tiles = {}
        pl_tiles = {}
        grp_tiles = {}
        cod_tiles = {}
        pa_tiles = {}
        agrp_tiles = {}
        acod_tiles = {}
        py_tiles = {}
        xc_tiles = {}
        xs_tiles = {}
        ag_tiles = {}

        def issue_s(k, t):
            gi, c = divmod(k, NCHUNK)
            b, gp = divmod(gi, 2)
            ps = ps_s.tile([P, NCH], F32, name="ps", tag="s")
            nc.tensor.matmul(ps[:], lhsT=nphiT[b][:, gp * 4 + t, :], rhs=thetaT[b][:, c * NCH:(c + 1) * NCH],
                             start=True, stop=True)
            ps_tiles[(k, t)] = ps

        def red_exp(k, t):
            gi, c = divmod(k, NCHUNK)
            if c == 0 and t == 0:
                nm_tiles[gi] = st_pool.tile([P, 4, NCHUNK], F32, name="nm", tag="nm")
                sm_tiles[gi] = st_pool.tile([P, 4, NCHUNK], F32, name="sm", tag="sm")
            if t == 0:
                e_tiles[k] = e_pool.tile([P, 4, NCH], F32, name="e", tag="e")
            ps = ps_tiles[(k, t)]
            nm = nm_tiles[gi]
            nc.vector.tensor_reduce(out=nm[:, t, c:c + 1], in_=ps[:], axis=AX.X, op=ALU.min)
            nc.scalar.activation(out=e_tiles[k][:, t, :], in_=ps[:], func=ACT.Exp, bias=nm[:, t, c:c + 1], scale=-1.0,
                                 accum_out=sm_tiles[gi][:, t, c:c + 1])

        def stats1(gi):
            nm = nm_tiles[gi]
            negm = st_pool.tile([P, 4], F32, name="negm", tag="negm")
            nc.vector.tensor_reduce(out=negm[:], in_=nm[:], axis=AX.X, op=ALU.min)
            d = st_pool.tile([P, 4, NCHUNK], F32, name="d", tag="d")
            nc.vector.tensor_tensor(out=d[:], in0=negm[:].unsqueeze(2).to_broadcast([P, 4, NCHUNK]), in1=nm[:],
                                    op=ALU.subtract)
            f = st_pool.tile([P, 4, NCHUNK], F32, name="f", tag="f")
            nc.scalar.activation(out=f[:], in_=d[:], func=ACT.Exp)
            f_tiles[gi] = f

        def stats2(gi):
            f = f_tiles[gi]
            fs = st_pool.tile([P, 4, NCHUNK], F32, name="fs", tag="fs")
            nc.vector.tensor_tensor(out=fs[:], in0=f[:], in1=sm_tiles[gi][:], op=ALU.mult)
            tot = st_pool.tile([P, 4], F32, name="tot", tag="tot")
            nc.vector.tensor_reduce(out=tot[:], in_=fs[:], axis=AX.X, op=ALU.add)
            r = st_pool.tile([P, 4], F32, name="r", tag="r")
            nc.vector.reciprocal(out=r[:], in_=tot[:])
            sc = st_pool.tile([P, 4, NCHUNK], F32, name="sc", tag="sc")
            nc.vector.tensor_tensor(out=sc[:], in0=f[:], in1=r[:].unsqueeze(2).to_broadcast([P, 4, NCHUNK]),
                                    op=ALU.mult)
            sc_tiles[gi] = sc

        def planes(j, who):
            gi, c = divmod(j, NCHUNK)
            eng = norm_engine(gi, c)
            if eng == "A":
                return
            if j not in pl_tiles:
                pl_tiles[j] = pl_pool.tile([P, 4, NCH], BF16, name="pl", tag="pl")
            pl = pl_tiles[j]
            e = e_tiles[j]
            sc = sc_tiles[gi]
            for t in range(4):
                if eng[t] not in who:
                    continue
                if eng[t] == "S":
                    nc.scalar.activation(out=pl[:, t, :], in_=e[:, t, :], func=ACT.Copy, scale=sc[:, t, c:c + 1])
                elif eng[t] == "G":
                    nc.gpsimd.tensor_scalar(out=pl[:, t, :], in0=e[:, t, :], scalar1=sc[:, t, c:c + 1],
                                            scalar2=0.0, op0=ALU.mult, op1=ALU.add)
                else:
                    nc.vector.tensor_scalar_mul(out=pl[:, t, :], in0=e[:, t, :], scalar1=sc[:, t, c:c + 1])

        def spans(j):
            return ((0, NCH // 2), (NCH // 2, NCH)) if j == NSTEP - NCHUNK else ((0, NCH),)

        def normalise(j):
            gi, c = divmod(j, NCHUNK)
            grp = grp_pool.tile([P, NCH, 4], BF16, name="grp", tag="grp", align_bytes=64)
            if norm_engine(gi, c) == "A":
                for n0, n1 in spans(j):
                    nc.vector.tensor_tensor(
                        out=grp[:, n0:n1, :].rearrange("p (c i) t -> p c t i", i=4),
                        in0=e_tiles[j][:, :, n0:n1].rearrange("p t (c i) -> p c t i", i=4),
                        in1=sc_tiles[gi][:, :, c:c + 1].unsqueeze(1).to_broadcast([P, (n1 - n0) // 4, 4, 4]),
                        op=ALU.mult,
                    )
            else:
                nc.vector.tensor_copy(
                    out=grp[:].rearrange("p (c i) t -> p c t i", i=4),
                    in_=pl_tiles[j][:].rearrange("p t (c i) -> p c t i", i=4),
                )
            grp_tiles[j] = grp

        def quantise(j):
            gi, c = divmod(j, NCHUNK)
            pool = cod0_pool if gi % 2 == 0 else cod1_pool
            cod = pool.tile([P, NCH], U32, name="cod", tag="cod", align_bytes=64)
            pln = pool.tile([P, NCH], U8, name="pln", tag="pln", align_bytes=64)
            for n0, n1 in spans(j):
                nc.vector.quantize_mx(out=cod[:, n0:n1].bitcast(FP8X4), scales=pln[:, n0:n1],
                                      in_=grp_tiles[j][:, n0:n1, :].rearrange("p n t -> p (n t)"))
            cod_tiles[j] = (cod, pln)

        def a_mm(j, sub):
            b = j // (2 * NCHUNK)
            ops = [cod_tiles[j - NCHUNK], cod_tiles[j]]
            if b == 0:
                pa = ps_a.tile([P, 4, P], F32, name="pa", tag="a")
            else:
                pa = ps_s.tile([P, 4, P], F32, name="pa", tag="s")
            cols = slice(sub * P, (sub + 1) * P)
            for jj in range(4):
                mcols = slice(jj * P, (jj + 1) * P)
                for gp in range(2):
                    nc.tensor.matmul_mx(
                        out=pa[:, jj, :],
                        lhsT=gcod[2 * b + gp][:, mcols].bitcast(FP8X4),
                        lhsT_scale=gpl[2 * b + gp][:, mcols],
                        rhs=ops[gp][0][:, cols].bitcast(FP8X4),
                        rhs_scale=ops[gp][1][:, cols],
                        start=(gp == 0),
                        stop=(gp == 1),
                    )
            pa_tiles[(j, sub)] = pa

        def on_vector(j, sub):
            return j >= NSTEP - 0 and sub >= 2

        def a_evac(j, sub):
            if sub == 0:
                agrp_tiles[j] = a_pool.tile([P, NCH, 4], BF16, name="agrp", tag="agrp", align_bytes=64)
            if on_vector(j, sub):
                nc.vector.tensor_copy(out=agrp_tiles[j][:, sub * P:(sub + 1) * P, :],
                                      in_=pa_tiles[(j, sub)][:].rearrange("p j n -> p n j"))
            else:
                nc.scalar.copy(out=agrp_tiles[j][:, sub * P:(sub + 1) * P, :],
                               in_=pa_tiles[(j, sub)][:].rearrange("p j n -> p n j"))

        def a_quant(j):
            acod = a_pool.tile([P, NCH], U32, name="acod", tag="acod", align_bytes=64)
            apl = a_pool.tile([P, NCH], U8, name="apl", tag="apl", align_bytes=64)
            nc.vector.quantize_mx(out=acod[:].bitcast(FP8X4), scales=apl[:],
                                  in_=agrp_tiles[j][:].rearrange("p n t -> p (n t)"))
            acod_tiles[j] = (acod, apl)

        def out_cols(j):
            c = j % NCHUNK
            return j // (2 * NCHUNK), slice(c * NCH, (c + 1) * NCH)

        def x_load(j):
            b, cols = out_cols(j)
            xc = x_pool.tile([P, NCH], BF16, name="xc", tag="xc")
            nc.sync.dma_start(out=xc[:], in_=x_v[b][:, cols])
            xc_tiles[j] = xc

        def x_scale(j):
            xs = io_pool.tile([P, NCH], F32, name="xs", tag="xs", bufs=3)
            if XS_ENGINE == "G" or (XS_ENGINE == "M" and j < 2 * NCHUNK):
                nc.gpsimd.tensor_scalar(out=xs[:], in0=xc_tiles[j][:], scalar1=oma[:, 0:1], scalar2=0.0, op0=ALU.mult,
                                        op1=ALU.add)
            else:
                nc.vector.tensor_scalar_mul(out=xs[:], in0=xc_tiles[j][:], scalar1=oma[:, 0:1])
            xs_tiles[j] = xs

        def y_mm(j):
            acod, apl = acod_tiles[j]
            py = ps_y.tile([P, NCH], F32, name="py", tag="y")
            nc.tensor.matmul_mx(out=py[:], lhsT=wcod[:].bitcast(FP8X4), lhsT_scale=wpl[:],
                                rhs=acod[:].bitcast(FP8X4), rhs_scale=apl[:], start=True, stop=True)
            py_tiles[j] = py

        def y_evac(j):
            b, cols = out_cols(j)
            ag = io_pool.tile([P, NCH], F32, name="ag", tag="ag", bufs=6)
            nc.scalar.activation(out=ag[:], in_=py_tiles[j][:], func=ACT.Identity, bias=b32[:, 0:1], scale=1.0)
            nc.sync.dma_start(out=o1_v[b][:, cols], in_=ag[:])
            ag_tiles[j] = ag

        def out_combine(j):
            b, cols = out_cols(j)
            o = io_pool.tile([P, NCH], F32, name="o", tag="o", bufs=4)
            nc.vector.scalar_tensor_tensor(out=o[:], in0=ag_tiles[j][:], scalar=alpha[:, 0:1], in1=xs_tiles[j][:],
                                           op0=ALU.mult, op1=ALU.add)
            nc.sync.dma_start(out=o0_v[b][:, cols], in_=o[:])

        def valid(j):
            return 0 <= j < NSTEP

        def second(j):
            return valid(j) and (j // NCHUNK) % 2 == 1

        setup = {}
        for i4 in range(2, 8):
            setup[i4 - 2] = [("theta", 0, i4)]
        setup[6] = [("phi", 0, 1)]
        setup[7] = [("w", 0, 0)]
        setup[8] = [("phi", 1, 0)]
        setup[9] = [("phi", 1, 1)]
        for i4 in range(8):
            setup[7 + i4] = setup.get(7 + i4, []) + [("theta", 1, i4)]

        def step(k):
            j = k - LAG
            for what, sb, si in setup.get(k, []):
                if what == "theta":
                    transpose_theta(sb, si)
                elif what == "phi":
                    transpose_phi(sb, si)
                else:
                    transpose_w()
            if k < NCHUNK:
                load_theta(1, k)
            if second(j + 1):
                x_load(j + 1)
            for u in range(4):
                if second(j - 2):
                    a_mm(j - 2, u)
                if k < NSTEP:
                    red_exp(k, u)
                if second(j - 2) and not on_vector(j - 2, u):
                    a_evac(j - 2, u)
                if k + 1 < NSTEP:
                    issue_s(k + 1, u)
                if u == 1 and second(j - 4):
                    y_mm(j - 4)
            if k < NSTEP and k % NCHUNK == NCHUNK - 1:
                stats1(k // NCHUNK)
            if k >= NCHUNK and k % NCHUNK == 0 and k <= NSTEP:
                stats2(k // NCHUNK - 1)
            for what, sb, si in setup.get(k, []):
                if what == "theta":
                    evac_theta(sb, si, sb == 0)
                elif what == "phi":
                    evac_phi(sb, si)
                else:
                    evac_w()
            if k == 3:
                small_constants_s()
            if k == 5:
                small_constants_v()
            if k == 8:
                quant_w()
            if k in (4, 6, 10, 12):
                quant_g((4, 6, 10, 12).index(k))
            if k in (0, 1, 5, 7):
                regroup_g((0, 1, 5, 7).index(k))
            if k in (0, 1):
                load_g(k + 2)
            if valid(j - 1) and j - 1 != NSTEP - NCHUNK:
                quantise(j - 1)
            if second(j - 3):
                a_quant(j - 3)
                if j - 3 < 2 * NCHUNK:
                    x_scale(j - 3)
            if second(j - 5) and j - 5 < 2 * NCHUNK:
                out_combine(j - 5)
            if second(j - 7) and j - 7 >= 2 * NCHUNK:
                x_scale(j - 7)
                out_combine(j - 7)
            for u in range(4):
                if second(j - 2) and on_vector(j - 2, u):
                    a_evac(j - 2, u)
            if valid(j + 1) and (LAG > NCHUNK or (j + 1) % NCHUNK != 0):
                planes(j + 1, "v")
            if LAG == NCHUNK and valid(j) and j % NCHUNK == 0:
                planes(j, "vGS")
            if valid(j):
                normalise(j)
            if j == NSTEP - NCHUNK:
                quantise(j)
            if second(j - 4):
                y_evac(j - 4)
            if valid(j + 1) and (LAG > NCHUNK or (j + 1) % NCHUNK != 0):
                planes(j + 1, "GS")

        with tc.manual_schedule():
            nc.sync.dma_start(out=praw[0][:, 0, :, :], in_=ph_v[0][:, 0, :, :])
            load_theta(0, 0)
            load_theta(0, 1)
            nc.gpsimd.dma_start(out=gam[:], in_=gamma.partition_broadcast(P))
            nc.gpsimd.dma_start(out=braw[:], in_=b_attn_g.rearrange("(p o) -> p o", o=1))
            for c in range(2, NCHUNK):
                load_theta(0, c)
            nc.sync.dma_start(out=praw[0][:, 1, :, :], in_=ph_v[0][:, 1, :, :])
            nc.sync.dma_start(out=wraw[:], in_=w_attn_g)
            nc.sync.dma_start(out=praw[1][:], in_=ph_v[1])
            for i in range(2):
                load_g(i)
            transpose_phi(0, 0)
            evac_phi(0, 0)
            transpose_theta(0, 0)
            evac_theta(0, 0, False)
            for t in range(4):
                issue_s(0, t)
            transpose_theta(0, 1)
            evac_theta(0, 1, False)

            for k in range(PINNED):
                step(k)
        for k in range(PINNED, NSTEP + LAG + 8):
            step(k)
